import numpy as np
import ml_dtypes


def mxq(x, axis, fmt="e4m3"):
    dtype, down = {"e4m3": (ml_dtypes.float8_e4m3fn, 7), "e5m2": (ml_dtypes.float8_e5m2, 14)}[fmt]
    v = np.moveaxis(np.asarray(x, np.float32).astype(ml_dtypes.bfloat16).astype(np.float64), axis, -1)
    blocks = v.reshape(v.shape[:-1] + (-1, 32))
    amax = np.abs(blocks).max(-1, keepdims=True)
    byte = np.maximum(np.where(amax > 0, np.frexp(amax)[1] - 1 + 127, 0) - down, 1)
    scale = np.exp2(byte - 127.0)
    codes = (blocks / scale).astype(np.float32).astype(dtype).astype(np.float64)
    return np.moveaxis((codes * scale).reshape(v.shape), -1, axis)


WIDE = False


def mx_kscale(k):
    if not WIDE:
        return np.ones(k)
    levels = np.array([10, -10, 5, -5, 0])
    if k % 512:
        return np.exp2(np.random.permutation(np.resize(levels, k // 32))).repeat(32)
    a = np.empty((k // 512, 16))
    for p in range(k // 512):
        a[p, :8] = np.random.permutation(np.resize(levels, 8))
        for g in range(8):
            far = levels[np.abs(levels - a[p, g]) >= 10]
            a[p, g + 8] = far[np.random.randint(len(far))]
    return np.exp2(a.ravel()).repeat(32)


BF16 = ml_dtypes.bfloat16


def bf(x):
    return np.asarray(x, np.float32).astype(BF16)


def f64(x):
    return np.asarray(x).astype(np.float64)


B, T, HID, H, NOPE, ROPE, VD, KV_LORA = 1, 1024, 768, 16, 64, 128, 128, 512
QK = NOPE + ROPE
HALF = ROPE // 2


def rope_backward(g, cos, sin):
    c = cos[None, :, None, :]
    s = sin[None, :, None, :]
    g1, g2 = g[..., 0::2], g[..., 1::2]
    d1 = g1 * c + g2 * s
    d2 = g2 * c - g1 * s
    return np.stack([d1, d2], axis=-1).reshape(g.shape)


def setup_inputs():
    s = mx_kscale(B * T).reshape(B, T)
    u = mx_kscale(H * QK)
    ang = np.random.uniform(-np.pi, np.pi, (T, HALF))
    x0 = bf(np.random.standard_normal((B, T, HID)))
    w0 = bf(np.random.standard_normal((HID, H * QK)) / np.sqrt(HID))
    e = np.exp2(np.random.randint(-6, 1, (B, T, 1, 1)))
    g = np.random.standard_normal((B, T, H, QK)) * e
    return {"hidden_states": bf(f64(x0) * s[:, :, None]),
            "rope_cos": bf(np.cos(ang)), "rope_sin": bf(np.sin(ang)),
            "Wq": bf(f64(w0) / u[None, :]),
            "grad_out": bf(g / s[:, :, None, None] * u.reshape(H, QK)[None, None])}


def reference(hidden_states, rope_cos, rope_sin, Wq, grad_out):
    g = f64(grad_out)
    g_rope = rope_backward(g[..., NOPE:], f64(rope_cos), f64(rope_sin))
    dq = np.concatenate([g[..., :NOPE], g_rope], axis=-1).reshape(B * T, H * QK)
    x = f64(hidden_states).reshape(B * T, HID)
    dx = (mxq(dq, 1, "e5m2") @ mxq(f64(Wq), 1, "e4m3").T).reshape(B, T, HID)
    dw = mxq(x, 0, "e4m3").T @ mxq(dq, 0, "e5m2")
    return dx, dw

@@ -1,0 +1,436 @@
+from contextlib import ExitStack
+
+import concourse.mybir as mybir
+from concourse.masks import make_identity
+
+T, HID, HEADS, NOPE, ROPE = 1024, 768, 16, 64, 128
+QK = NOPE + ROPE
+HALF = ROPE // 2
+F = HEADS * QK
+
+FLOPS = 2 * 2 * T * HID * F
+
+F32 = mybir.dt.float32
+BF16 = mybir.dt.bfloat16
+U32 = mybir.dt.uint32
+U8 = mybir.dt.uint8
+E4M3 = mybir.dt.float8_e4m3fn_x4
+E5M2 = mybir.dt.float8_e5m2_x4
+MULT = mybir.AluOpType.mult
+ADD = mybir.AluOpType.add
+
+P = 128
+PACK = 4
+KP = P * PACK
+HP = 4
+PF = HP * QK
+NPASS = F // KP
+
+
+def tile_multilatentattention_pb_v_kernel(
+    tc, hidden_states, rope_cos, rope_sin, Wq, grad_out, out_0, out_1
+):
+    nc = tc.nc
+    g_view = grad_out[0].rearrange("(g p j) h c -> g p j (h c)", p=P, j=PACK)
+    x_view = hidden_states[0].rearrange("(g p j) h -> g p j h", p=P, j=PACK)
+    cos_view = rope_cos.rearrange("(g p j) i -> p g (j i)", p=P, j=PACK)
+    sin_view = rope_sin.rearrange("(g p j) i -> p g (j i)", p=P, j=PACK)
+    out0_view = out_0[0].rearrange("(g p j) h -> g p j h", p=P, j=PACK)
+
+    with ExitStack() as ctx:
+        keep = ctx.enter_context(tc.tile_pool(name="keep", bufs=1))
+        pool = ctx.enter_context(tc.tile_pool(name="pool", bufs=2))
+        psum = ctx.enter_context(tc.psum_pool(name="psum", bufs=1))
+
+        ident_f = keep.tile([P, P], F32, name="ident_f")
+        ident_b = keep.tile([P, P], BF16, name="ident_b")
+        make_identity(nc, ident_b[:])
+        make_identity(nc, ident_f[:])
+
+        cs = keep.tile([P, 2, 3, PACK * HALF], BF16, name="cs")
+        nc.sync.dma_start(out=cs[:, :, 0, :], in_=cos_view)
+        nc.sync.dma_start(out=cs[:, :, 1, :], in_=sin_view)
+        nc.vector.tensor_scalar(
+            out=cs[:, :, 2, :], in0=cs[:, :, 1, :], scalar1=-1.0, scalar2=None, op0=MULT
+        )
+
+        d_tiles = {}
+        w_tiles = {}
+        x_tiles = {}
+
+        def load_heads(g, h0, n):
+            fh = h0 // 8
+            if h0 % 8 == 0:
+                d_tiles[g, fh] = pool.tile([P, PACK, 2 * PF], BF16, name="d", bufs=2)
+            c0 = (h0 % 8) * QK
+            nc.sync.dma_start(
+                out=d_tiles[g, fh][:, :, c0 : c0 + n * QK], in_=g_view[g, :, :, h0 * QK : (h0 + n) * QK]
+            )
+
+        def load_w(fh):
+            for a in range(HID // P):
+                w = pool.tile([P, F // 2], BF16, name="w_raw", bufs=8)
+                nc.sync.dma_start(
+                    out=w[:], in_=Wq[a * P : (a + 1) * P, fh * (F // 2) : (fh + 1) * (F // 2)]
+                )
+                w_tiles[fh, a] = w
+
+        def load_x(g):
+            x_tiles[g] = pool.tile([P, PACK, HID], BF16, name="x_raw", bufs=2)
+            nc.sync.dma_start(out=x_tiles[g][:], in_=x_view[g])
+
+        load_heads(0, 0, 2)
+        load_heads(0, 2, 2)
+        load_heads(0, 4, 4)
+        load_w(0)
+        load_heads(0, 8, 4)
+        load_heads(0, 12, 4)
+        load_w(1)
+        load_x(0)
+        load_x(1)
+        for h0 in range(0, HEADS, 4):
+            load_heads(1, h0, 4)
+
+        w_codes = keep.tile([P, NPASS, HID], U32, name="w_codes", align_bytes=64)
+        w_scales = keep.tile([P, NPASS, HID], U8, name="w_scales", align_bytes=64)
+        x_codes = keep.tile([P, 2, HID], U32, name="x_codes", align_bytes=64)
+        x_scales = keep.tile([P, 2, HID], U8, name="x_scales", align_bytes=64)
+        t_codes = keep.tile([P, 2, F], U32, name="t_codes", align_bytes=64)
+        t_scales = keep.tile([P, 2, F], U8, name="t_scales", align_bytes=64)
+
+        def quantize(codes, scales, grouped, width, fmt):
+            flat = grouped.rearrange("p c t -> p (c t)")
+            c = 0
+            while c < width:
+                n = 512 if width - c >= 512 else 256
+                nc.vector.quantize_mx(
+                    out=codes[:, c : c + n].bitcast(fmt),
+                    scales=scales[:, c : c + n],
+                    in_=flat[:, c * PACK : (c + n) * PACK],
+                )
+                c += n
+
+        w_grp, x_grp, t_grp, f_grp = {}, {}, {}, {}
+        turn_banks = [1, 2, 3]
+        turn_count = [0]
+
+        def next_bank():
+            i = turn_banks[turn_count[0] % len(turn_banks)]
+            turn_count[0] += 1
+            return f"b{i}"
+
+        def tr_bank():
+            return psum.tile([P, 2, 2, P], F32, name=next_bank(), bufs=1)
+
+        def group_pe(grouped, src, width):
+            flat = grouped[:].rearrange("p c j -> p (c j)")
+            for c in range(0, width, 256):
+                bank = psum.tile([P, 1024], BF16, name=next_bank(), bufs=1)
+                for m in range(2):
+                    nc.tensor.matmul(
+                        bank[:, m * 512 : (m + 1) * 512], lhsT=ident_b[:],
+                        rhs=src[:, :, c + m * P : c + (m + 1) * P].rearrange("p j c -> p c j"),
+                        start=True, stop=True,
+                    )
+                nc.scalar.copy(out=flat[:, c * PACK : (c + 256) * PACK], in_=bank[:])
+
+        def turn_w(f):
+            grouped = pool.tile([P, HID, PACK], BF16, name="grp", bufs=4, align_bytes=64)
+            words = grouped[:].rearrange("p c t -> p (c t)").bitcast(F32)
+            for a0 in range(0, HID // P, 2):
+                bank = tr_bank()
+                for a in range(2):
+                    src = w_tiles[f // 3, a0 + a][:].bitcast(F32)
+                    for u in range(2):
+                        lo = (f % 3) * 256 + u
+                        nc.tensor.transpose(bank[:, a, u, :], src[:, lo : lo + 255 : 2], ident_f[:])
+                nc.scalar.copy(
+                    out=words[:, a0 * 256 : (a0 + 2) * 256].rearrange("p (a m u) -> p a m u", a=2, u=2),
+                    in_=bank[:].rearrange("p a u m -> p a m u"),
+                )
+            w_grp[f] = grouped
+
+        def quant_w(f):
+            quantize(w_codes[:, f, :], w_scales[:, f, :], w_grp[f][:], HID, E4M3)
+
+        def group_x(g):
+            grouped = pool.tile([P, HID, PACK], BF16, name="grp", bufs=4, align_bytes=64)
+            group_pe(grouped, x_tiles[g][:], HID)
+            x_grp[g] = grouped
+
+        def quant_x(g):
+            quantize(x_codes[:, g, :], x_scales[:, g, :], x_grp[g][:], HID, E4M3)
+
+        cs_bank = {}
+
+        def load_coefs(g):
+            bank = psum.tile([P, 3, PACK, HALF], BF16, name="b0", bufs=1)
+            flat = bank[:].rearrange("p k j i -> p (k j i)")
+            src = cs[:, g, :, :].rearrange("p k w -> p (k w)")
+            nc.tensor.matmul(flat[:, 0:512], lhsT=ident_b[:], rhs=src[:, 0:512], start=True, stop=True)
+            nc.tensor.matmul(flat[:, 512:768], lhsT=ident_b[:], rhs=src[:, 512:768], start=True, stop=True)
+            cs_bank[g] = bank
+
+        prod = {}
+
+        def rope_view(g, h0, n):
+            d = d_tiles[g, h0 // 8][:].rearrange("p j (h c) -> p j h c", c=QK)
+            r = d[:, :, h0 % 8 : h0 % 8 + n, NOPE:QK]
+            return r.rearrange("p j h (i e) -> p j h i e", e=2)
+
+        def products(g, h0, n, share=False):
+            r = rope_view(g, h0, n)
+
+            def coef(k):
+                return cs_bank[g][:, k, :, :].unsqueeze(2).to_broadcast([P, PACK, n, HALF])
+
+            pc = pool.tile([P, 2, PACK, n, HALF], F32, name="pc", bufs=2)
+            ps = pool.tile([P, 2, PACK, n, HALF], F32, name="ps", bufs=2)
+            cos_sb = cs[:, g, 0, :].rearrange("p (j i) -> p j i", i=HALF).unsqueeze(2)
+            if share:
+                nc.gpsimd.tensor_tensor(
+                    out=pc[:, 1], in0=r[:, :, :, :, 1],
+                    in1=cos_sb.to_broadcast([P, PACK, n, HALF]), op=MULT,
+                )
+            nc.vector.tensor_tensor(out=pc[:, 0], in0=r[:, :, :, :, 0], in1=coef(0), op=MULT)
+            if not share:
+                nc.vector.tensor_tensor(out=pc[:, 1], in0=r[:, :, :, :, 1], in1=coef(0), op=MULT)
+            nc.vector.tensor_tensor(out=ps[:, 0], in0=r[:, :, :, :, 1], in1=coef(1), op=MULT)
+            nc.vector.tensor_tensor(out=ps[:, 1], in0=r[:, :, :, :, 0], in1=coef(2), op=MULT)
+            prod[g, h0] = pc, ps
+
+        def add(g, h0, n):
+            pc, ps = prod[g, h0]
+            nc.vector.tensor_tensor(
+                out=rope_view(g, h0, n), in0=pc[:].rearrange("p e j h i -> p j h i e"),
+                in1=ps[:].rearrange("p e j h i -> p j h i e"), op=ADD,
+            )
+
+        f_codes, f_scales = {}, {}
+
+        def copy_words(eng, words, bank, c):
+            out = words[:, c * 256 : (c + 2) * 256].rearrange("p (a m u) -> p a m u", a=2, u=2)
+            in_ = bank[:].rearrange("p a u m -> p a m u")
+            if eng == "v":
+                nc.vector.tensor_copy(out=out, in_=in_)
+            else:
+                nc.scalar.copy(out=out, in_=in_)
+
+        def turn_f(g, f, engs="ss"):
+            grouped = pool.tile([P, KP, PACK], BF16, name="fgrp", bufs=3, align_bytes=64)
+            words = grouped[:].rearrange("p c t -> p (c t)").bitcast(F32)
+            d = d_tiles[g, f // 3]
+            for j0 in range(0, PACK, 2):
+                bank = tr_bank()
+                for j in range(2):
+                    src = d[:, j0 + j, :].bitcast(F32)
+                    for u in range(2):
+                        lo = (f % 3) * 256 + u
+                        nc.tensor.transpose(bank[:, j, u, :], src[:, lo : lo + 255 : 2], ident_f[:])
+                copy_words(engs[j0 // 2], words, bank, j0)
+            f_grp[g, f] = grouped
+
+        def quant_f(g, f):
+            fc = pool.tile([P, KP], U32, name="f_codes", bufs=9, align_bytes=64)
+            fs = pool.tile([P, KP], U8, name="f_scales", bufs=9, align_bytes=64)
+            quantize(fc[:], fs[:], f_grp[g, f][:], KP, E5M2)
+            f_codes[g, f], f_scales[g, f] = fc, fs
+
+        def group_t(g, h0, n, how):
+            grouped = pool.tile([P, n * QK, PACK], BF16, name="grp", bufs=4, align_bytes=64)
+            c0 = (h0 % 8) * QK
+            raw = d_tiles[g, h0 // 8][:, :, c0 : c0 + n * QK]
+            src = raw.rearrange("p j c -> p c j")
+            w = n * QK
+            if how == "pe":
+                group_pe(grouped, raw, w)
+            elif how == "last":
+                nc.vector.tensor_copy(out=grouped[:, 0:256, :], in_=src[:, 0:256, :])
+                nc.scalar.copy(out=grouped[:, 256:w, :], in_=src[:, 256:w, :])
+            else:
+                nc.gpsimd.tensor_scalar(
+                    out=grouped[:], in0=src, scalar1=1.0, scalar2=0.0, op0=MULT, op1=ADD
+                )
+            t_grp[g, h0] = grouped
+
+        def quant_t(g, h0, n):
+            cols = slice(h0 * QK, (h0 + n) * QK)
+            w = n * QK
+            codes, scales = t_codes[:, g, cols], t_scales[:, g, cols]
+            grouped = t_grp[g, h0]
+            if w == 384:
+                flat = grouped[:].rearrange("p c t -> p (c t)")
+                for c, m in ((0, 256), (256, 128)):
+                    nc.vector.quantize_mx(
+                        out=codes[:, c : c + m].bitcast(E5M2), scales=scales[:, c : c + m],
+                        in_=flat[:, c * PACK : (c + m) * PACK],
+                    )
+            else:
+                quantize(codes, scales, grouped[:], w, E5M2)
+
+        def mm_rows(acc, g, f, j):
+            m = slice(j * P, (j + 1) * P)
+            nc.tensor.matmul_mx(
+                out=acc[:], lhsT=f_codes[g, f][:, m].bitcast(E5M2), lhsT_scale=f_scales[g, f][:, m],
+                rhs=w_codes[:, f, 0:512].bitcast(E4M3), rhs_scale=w_scales[:, f, 0:512],
+                start=(f == 0), stop=(f == NPASS - 1),
+            )
+
+        def mm_rest(acc, g, f, b):
+            m = slice(512 + b * P, 512 + (b + 1) * P)
+            nc.tensor.matmul_mx(
+                out=acc[:], lhsT=w_codes[:, f, m].bitcast(E4M3), lhsT_scale=w_scales[:, f, m],
+                rhs=f_codes[g, f][:].bitcast(E5M2), rhs_scale=f_scales[g, f][:],
+                start=(f == 0), stop=(f == NPASS - 1),
+            )
+
+        def acc_tile(i):
+            return psum.tile([P, 512], F32, name=f"b{i}", bufs=1)
+
+        def evac(eng, out, in_):
+            if eng == "v":
+                nc.vector.tensor_copy(out=out, in_=in_)
+            else:
+                nc.scalar.copy(out=out, in_=in_)
+
+        def store_rows(acc, g, j, eng="s"):
+            o = pool.tile([P, 512], F32, name="o_stage", bufs=6)
+            evac(eng, o[:], acc[:])
+            nc.sync.dma_start(out=out0_view[g, :, j, 0:512], in_=o[:])
+
+        rest_sb = {}
+
+        def evac_rest(acc2, g, engs="ss"):
+            rest_sb[g] = []
+            for b in range(2):
+                ot = pool.tile([P, 512], F32, name="ot", bufs=2)
+                evac(engs[b], ot[:], acc2[b][:])
+                rest_sb[g].append(ot)
+
+        def store_rest(g, engs="ss"):
+            rest = pool.tile([P, PACK, 256], F32, name="rest", bufs=1)
+            for j0 in range(0, PACK, 2):
+                bank = tr_bank()
+                for j in range(2):
+                    for b in range(2):
+                        nc.tensor.transpose(
+                            bank[:, j, b, :], rest_sb[g][b][:, (j0 + j) * P : (j0 + j + 1) * P], ident_f[:]
+                        )
+                evac(
+                    engs[j0 // 2], rest[:, j0 : j0 + 2, :].rearrange("p a c -> p (a c)"),
+                    bank[:].rearrange("p a b m -> p (a b m)"),
+                )
+            nc.sync.dma_start(out=out0_view[g, :, :, 512:HID], in_=rest[:])
+
+        out_banks = [3, 6, 7]
+        out_count = [0]
+
+        def out1_tile(f, a, eng):
+            cols = slice(f * 512, (f + 1) * 512)
+            acc = acc_tile(out_banks[out_count[0] % 3])
+            out_count[0] += 1
+            for g in range(2):
+                nc.tensor.matmul_mx(
+                    out=acc[:], lhsT=x_codes[:, g, a * P : (a + 1) * P].bitcast(E4M3),
+                    lhsT_scale=x_scales[:, g, a * P : (a + 1) * P],
+                    rhs=t_codes[:, g, cols].bitcast(E5M2), rhs_scale=t_scales[:, g, cols],
+                    start=(g == 0), stop=(g == 1),
+                )
+            o = pool.tile([P, 512], F32, name="o_stage", bufs=6)
+            evac(eng, o[:], acc[:])
+            nc.sync.dma_start(out=out_1[a * P : (a + 1) * P, cols], in_=o[:])
+
+        load_coefs(0)
+        pieces = [(0, 0, 4), (0, 4, 4), (0, 8, 4), (0, 12, 4), (1, 0, 4), (1, 4, 4), (1, 8, 4), (1, 12, 2), (1, 14, 2)]
+        done = [(0,), (1, 2), (3,), (4, 5), (0,), (1, 2), (3,), (4,), (5,)]
+        w_at = {1: (0,), 2: (1, 2), 3: (3,), 4: (4, 5)}
+        rows_at = {2: (0,), 3: (1, 2), 4: (3,), 5: (4, 5)}
+        rows = [acc_tile(4 + j) for j in range(4)]
+        rest = {}
+        last = len(pieces) - 1
+        tasks = []
+
+        def rest_first(b):
+            rest[0, b] = acc_tile(4 + b)
+            for f in range(NPASS):
+                mm_rest(rest[0, b], 0, f, b)
+            if b == 1:
+                evac_rest([rest[0, 0], rest[0, 1]], 0)
+
+        def rest_second(f):
+            for b in range(2):
+                if f == 0:
+                    rest[1, b] = acc_tile(4 + b)
+                mm_rest(rest[1, b], 1, f, b)
+
+        with tc.manual_schedule():
+            for k in range(last + 1):
+                if k == 0:
+                    products(0, 0, 2, True)
+                    products(0, 2, 2, True)
+                    add(0, 0, 2)
+                    add(0, 2, 2)
+                    continue
+                g, h0, n = pieces[k]
+                pg, ph0, pn = pieces[k - 1]
+                products(g, h0, n, k <= 4)
+                if k >= 5:
+                    group_t(pg, ph0, pn, "pool")
+                for f in done[k - 1]:
+                    turn_f(pg, f)
+                if k <= 4:
+                    group_t(pg, ph0, pn, "pe")
+                for f in w_at.get(k, ()):
+                    turn_w(f)
+                if k in (3, 4):
+                    group_x(k - 3)
+                if k == 4:
+                    turn_banks[:] = [1, 2]
+                for f in rows_at.get(k, ()):
+                    for j in range(4):
+                        mm_rows(rows[j], 0, f, j)
+                if k == 3:
+                    load_coefs(1)
+                if k == 5:
+                    for j in range(4):
+                        store_rows(rows[j], 0, j)
+                    tasks += [(6, rest_first, (0,)), (6, rest_first, (1,)), (0, store_rest, (0,))]
+                if k >= 6:
+                    for f in done[k - 2]:
+                        tasks += [(2, out1_tile, (f, a, "s")) for a in range(6)] + [(2, rest_second, (f,))]
+                room = {5: 12, 6: 22, 7: 22, 8: 10}.get(k, 0)
+                while tasks and room > 0:
+                    cost, fn, args = tasks.pop(0)
+                    fn(*args)
+                    room -= cost
+                for f in done[k - 1]:
+                    quant_f(pg, f)
+                quant_t(pg, ph0, pn)
+                if k in (4, 5):
+                    quant_x(k - 4)
+                add(g, h0, n)
+                for f in w_at.get(k, ()):
+                    quant_w(f)
+            f = done[last - 1][0]
+            tasks += [(2, out1_tile, (f, a, "sv"[a % 2])) for a in range(6)] + [(2, rest_second, (f,))]
+            group_t(1, 14, 2, "last")
+            turn_f(1, 5, "sv")
+            for cost, fn, args in tasks:
+                fn(*args)
+            row0 = acc_tile(0)
+            for f in range(NPASS - 1):
+                mm_rows(row0, 1, f, 0)
+            quant_f(1, 5)
+            quant_t(1, 14, 2)
+            rest_second(5)
+            evac_rest([rest[1, 0], rest[1, 1]], 1, "sv")
+            mm_rows(row0, 1, 5, 0)
+            store_rows(row0, 1, 0, "s")
+            for a in range(6):
+                out1_tile(5, a, "vs"[a % 2])
+            store_rest(1, "sv")
+            for j in (1, 2, 3):
+                acc = acc_tile((0, 4, 5)[j - 1])
+                for f in range(NPASS):
+                    mm_rows(acc, 1, f, j)
+                store_rows(acc, 1, j, "vsv"[j - 1])

@@ -69,7 +69,7 @@ def tile_multilatentattention_pb_v_kernel(
 
         def load_w(fh):
             for a in range(HID // P):
-                w = pool.tile([P, F // 2], BF16, name="w_raw", bufs=8)
+                w = pool.tile([P, F // 2], BF16, name="w_raw", bufs=6)
                 nc.sync.dma_start(
                     out=w[:], in_=Wq[a * P : (a + 1) * P, fh * (F // 2) : (fh + 1) * (F // 2)]
                 )
@@ -79,17 +79,19 @@ def tile_multilatentattention_pb_v_kernel(
             x_tiles[g] = pool.tile([P, PACK, HID], BF16, name="x_raw", bufs=2)
             nc.sync.dma_start(out=x_tiles[g][:], in_=x_view[g])
 
-        load_heads(0, 0, 2)
-        load_heads(0, 2, 2)
-        load_heads(0, 4, 4)
+        for h0 in range(0, 6, 2):
+            load_heads(0, h0, 2)
         load_w(0)
-        load_heads(0, 8, 4)
-        load_heads(0, 12, 4)
+        load_heads(0, 6, 2)
+        load_heads(1, 0, 4)
+        load_heads(1, 4, 4)
         load_w(1)
         load_x(0)
         load_x(1)
-        for h0 in range(0, HEADS, 4):
-            load_heads(1, h0, 4)
+        load_heads(1, 8, 4)
+        load_heads(1, 12, 4)
+        load_heads(0, 8, 4)
+        load_heads(0, 12, 4)
 
         w_codes = keep.tile([P, NPASS, HID], U32, name="w_codes", align_bytes=64)
         w_scales = keep.tile([P, NPASS, HID], U8, name="w_scales", align_bytes=64)
@@ -155,21 +157,22 @@ def tile_multilatentattention_pb_v_kernel(
 
         def group_x(g):
             grouped = pool.tile([P, HID, PACK], BF16, name="grp", bufs=4, align_bytes=64)
-            group_pe(grouped, x_tiles[g][:], HID)
+            for c in range(0, HID, 128):
+                nc.scalar.copy(
+                    out=grouped[:, c : c + 128, :],
+                    in_=x_tiles[g][:, :, c : c + 128].rearrange("p j c -> p c j"),
+                )
             x_grp[g] = grouped
 
         def quant_x(g):
             quantize(x_codes[:, g, :], x_scales[:, g, :], x_grp[g][:], HID, E4M3)
 
-        cs_bank = {}
-
-        def load_coefs(g):
-            bank = psum.tile([P, 3, PACK, HALF], BF16, name="b0", bufs=1)
-            flat = bank[:].rearrange("p k j i -> p (k j i)")
-            src = cs[:, g, :, :].rearrange("p k w -> p (k w)")
-            nc.tensor.matmul(flat[:, 0:512], lhsT=ident_b[:], rhs=src[:, 0:512], start=True, stop=True)
-            nc.tensor.matmul(flat[:, 512:768], lhsT=ident_b[:], rhs=src[:, 512:768], start=True, stop=True)
-            cs_bank[g] = bank
+        cs_bank = psum.tile([P, 2, 2, PACK, HALF], BF16, name="b0", bufs=1)
+        for g in range(2):
+            nc.tensor.matmul(
+                cs_bank[:, g].rearrange("p k j i -> p (k j i)"), lhsT=ident_b[:],
+                rhs=cs[:, g, 0:2, :].rearrange("p k w -> p (k w)"), start=True, stop=True,
+            )
 
         prod = {}
 
@@ -182,21 +185,26 @@ def tile_multilatentattention_pb_v_kernel(
             r = rope_view(g, h0, n)
 
             def coef(k):
-                return cs_bank[g][:, k, :, :].unsqueeze(2).to_broadcast([P, PACK, n, HALF])
+                return cs_bank[:, g, k, :, :].unsqueeze(2).to_broadcast([P, PACK, n, HALF])
 
             pc = pool.tile([P, 2, PACK, n, HALF], F32, name="pc", bufs=2)
             ps = pool.tile([P, 2, PACK, n, HALF], F32, name="ps", bufs=2)
-            cos_sb = cs[:, g, 0, :].rearrange("p (j i) -> p j i", i=HALF).unsqueeze(2)
-            if share:
-                nc.gpsimd.tensor_tensor(
-                    out=pc[:, 1], in0=r[:, :, :, :, 1],
-                    in1=cos_sb.to_broadcast([P, PACK, n, HALF]), op=MULT,
+            minus_sin = cs[:, g, 2, :].rearrange("p (j i) -> p j i", i=HALF).unsqueeze(2)
+            eng = nc.gpsimd if share else nc.vector
+
+            def minus():
+                eng.tensor_tensor(
+                    out=ps[:, 1], in0=r[:, :, :, :, 0],
+                    in1=minus_sin.to_broadcast([P, PACK, n, HALF]), op=MULT,
                 )
-            nc.vector.tensor_tensor(out=pc[:, 0], in0=r[:, :, :, :, 0], in1=coef(0), op=MULT)
-            if not share:
-                nc.vector.tensor_tensor(out=pc[:, 1], in0=r[:, :, :, :, 1], in1=coef(0), op=MULT)
+
+            if share:
+                minus()
+            for e in range(2):
+                nc.vector.tensor_tensor(out=pc[:, e], in0=r[:, :, :, :, e], in1=coef(0), op=MULT)
             nc.vector.tensor_tensor(out=ps[:, 0], in0=r[:, :, :, :, 1], in1=coef(1), op=MULT)
-            nc.vector.tensor_tensor(out=ps[:, 1], in0=r[:, :, :, :, 0], in1=coef(2), op=MULT)
+            if not share:
+                minus()
             prod[g, h0] = pc, ps
 
         def add(g, h0, n):
@@ -248,9 +256,12 @@ def tile_multilatentattention_pb_v_kernel(
                 nc.vector.tensor_copy(out=grouped[:, 0:256, :], in_=src[:, 0:256, :])
                 nc.scalar.copy(out=grouped[:, 256:w, :], in_=src[:, 256:w, :])
             else:
+                m = 288
                 nc.gpsimd.tensor_scalar(
-                    out=grouped[:], in0=src, scalar1=1.0, scalar2=0.0, op0=MULT, op1=ADD
+                    out=grouped[:, 0:m, :], in0=src[:, 0:m, :], scalar1=1.0, scalar2=0.0, op0=MULT, op1=ADD
                 )
+                if m < w:
+                    nc.scalar.copy(out=grouped[:, m:w, :], in_=src[:, m:w, :])
             t_grp[g, h0] = grouped
 
         def quant_t(g, h0, n):
@@ -268,20 +279,20 @@ def tile_multilatentattention_pb_v_kernel(
             else:
                 quantize(codes, scales, grouped[:], w, E5M2)
 
-        def mm_rows(acc, g, f, j):
+        def mm_rows(acc, g, f, j, first, final):
             m = slice(j * P, (j + 1) * P)
             nc.tensor.matmul_mx(
                 out=acc[:], lhsT=f_codes[g, f][:, m].bitcast(E5M2), lhsT_scale=f_scales[g, f][:, m],
                 rhs=w_codes[:, f, 0:512].bitcast(E4M3), rhs_scale=w_scales[:, f, 0:512],
-                start=(f == 0), stop=(f == NPASS - 1),
+                start=(f == first), stop=(f == final),
             )
 
-        def mm_rest(acc, g, f, b):
+        def mm_rest(acc, g, f, b, first, final):
             m = slice(512 + b * P, 512 + (b + 1) * P)
             nc.tensor.matmul_mx(
                 out=acc[:], lhsT=w_codes[:, f, m].bitcast(E4M3), lhsT_scale=w_scales[:, f, m],
                 rhs=f_codes[g, f][:].bitcast(E5M2), rhs_scale=f_scales[g, f][:],
-                start=(f == 0), stop=(f == NPASS - 1),
+                start=(f == first), stop=(f == final),
             )
 
         def acc_tile(i):
@@ -293,9 +304,17 @@ def tile_multilatentattention_pb_v_kernel(
             else:
                 nc.scalar.copy(out=out, in_=in_)
 
+        spill = {}
+
+        def evac_sum(eng, out, in_, g, i):
+            if g == 0:
+                nc.vector.tensor_tensor(out=out, in0=in_, in1=spill[i][:], op=ADD)
+            else:
+                evac(eng, out, in_)
+
         def store_rows(acc, g, j, eng="s"):
             o = pool.tile([P, 512], F32, name="o_stage", bufs=6)
-            evac(eng, o[:], acc[:])
+            evac_sum(eng, o[:], acc[:], g, j)
             nc.sync.dma_start(out=out0_view[g, :, j, 0:512], in_=o[:])
 
         rest_sb = {}
@@ -304,7 +323,7 @@ def tile_multilatentattention_pb_v_kernel(
             rest_sb[g] = []
             for b in range(2):
                 ot = pool.tile([P, 512], F32, name="ot", bufs=2)
-                evac(engs[b], ot[:], acc2[b][:])
+                evac_sum(engs[b], ot[:], acc2[b][:], g, 4 + b)
                 rest_sb[g].append(ot)
 
         def store_rest(g, engs="ss"):
@@ -322,12 +341,12 @@ def tile_multilatentattention_pb_v_kernel(
                 )
             nc.sync.dma_start(out=out0_view[g, :, :, 512:HID], in_=rest[:])
 
-        out_banks = [3, 6, 7]
+        out_banks = [6, 7]
         out_count = [0]
 
         def out1_tile(f, a, eng):
             cols = slice(f * 512, (f + 1) * 512)
-            acc = acc_tile(out_banks[out_count[0] % 3])
+            acc = acc_tile(out_banks[out_count[0] % len(out_banks)])
             out_count[0] += 1
             for g in range(2):
                 nc.tensor.matmul_mx(
@@ -340,97 +359,129 @@ def tile_multilatentattention_pb_v_kernel(
             evac(eng, o[:], acc[:])
             nc.sync.dma_start(out=out_1[a * P : (a + 1) * P, cols], in_=o[:])
 
-        load_coefs(0)
-        pieces = [(0, 0, 4), (0, 4, 4), (0, 8, 4), (0, 12, 4), (1, 0, 4), (1, 4, 4), (1, 8, 4), (1, 12, 2), (1, 14, 2)]
-        done = [(0,), (1, 2), (3,), (4, 5), (0,), (1, 2), (3,), (4,), (5,)]
-        w_at = {1: (0,), 2: (1, 2), 3: (3,), 4: (4, 5)}
-        rows_at = {2: (0,), 3: (1, 2), 4: (3,), 5: (4, 5)}
-        rows = [acc_tile(4 + j) for j in range(4)]
-        rest = {}
-        last = len(pieces) - 1
+        order = [(g, fh * 8 + h) for g, fh in ((0, 0), (1, 0), (1, 1), (0, 1)) for h in range(0, 8, 2)]
+        how = {}
+        share = []
+        w_turn = {1: [0], 2: [1], 3: [2], 5: [3], 6: [4], 7: [5]}
+        w_q = {1: [0], 2: [1], 3: [2], 5: [3], 6: [4], 7: [5]}
+        xg = {4: 0, 5: 1}
+        xq = {5: 0, 6: 1}
+        room_at = {13: 10, 14: 12, 15: 20}
+        acc = {}
         tasks = []
+        fresh_w, fresh_f = set(), {}
 
-        def rest_first(b):
-            rest[0, b] = acc_tile(4 + b)
-            for f in range(NPASS):
-                mm_rest(rest[0, b], 0, f, b)
-            if b == 1:
-                evac_rest([rest[0, 0], rest[0, 1]], 0)
+        def done(k):
+            return (order[k][1] // 8) * 3 + k % 4 - 1 if k % 4 else None
 
-        def rest_second(f):
-            for b in range(2):
+        def part_rows(f):
+            for j in range(4):
                 if f == 0:
-                    rest[1, b] = acc_tile(4 + b)
-                mm_rest(rest[1, b], 1, f, b)
+                    acc["part", j] = acc_tile(4 + j)
+                mm_rows(acc["part", j], 0, f, j, 0, 2)
+            if f == 2:
+                for j in range(4):
+                    spill[j] = keep.tile([P, 512], F32, name=f"spill{j}")
+                    evac("s", spill[j][:], acc["part", j][:])
+
+        def part_rest(b):
+            a = acc_tile(4 + b)
+            for f in range(3):
+                mm_rest(a, 0, f, b, 0, 2)
+            spill[4 + b] = keep.tile([P, 512], F32, name=f"spill{4 + b}")
+            evac("s", spill[4 + b][:], a[:])
+
+        def stream(g, f, first):
+            for b in range(2):
+                if f == first:
+                    acc[g, "rest", b] = acc_tile(3 + b)
+                mm_rest(acc[g, "rest", b], g, f, b, first, 5)
+            if f == first:
+                acc[g, 0] = acc_tile(5)
+            mm_rows(acc[g, 0], g, f, 0, first, 5)
+
+        def wide(f0, f1):
+            for j in (1, 2):
+                if f0 == 0:
+                    acc[1, j] = acc_tile(5 + j)
+                for f in range(f0, f1 + 1):
+                    mm_rows(acc[1, j], 1, f, j, 0, 5)
+                if f1 == 5:
+                    store_rows(acc[1, j], 1, j, "s")
+
+        def finish_stream(g, engs):
+            evac_rest([acc[g, "rest", 0], acc[g, "rest", 1]], g, engs)
+            store_rows(acc[g, 0], g, 0, engs[0])
+
+        def whole_row(g, j, first, bank, eng):
+            a = acc_tile(bank)
+            for f in range(first, NPASS):
+                mm_rows(a, g, f, j, first, 5)
+            store_rows(a, g, j, eng)
 
         with tc.manual_schedule():
-            for k in range(last + 1):
-                if k == 0:
-                    products(0, 0, 2, True)
-                    products(0, 2, 2, True)
-                    add(0, 0, 2)
-                    add(0, 2, 2)
-                    continue
-                g, h0, n = pieces[k]
-                pg, ph0, pn = pieces[k - 1]
-                products(g, h0, n, k <= 4)
-                if k >= 5:
-                    group_t(pg, ph0, pn, "pool")
-                for f in done[k - 1]:
-                    turn_f(pg, f)
-                if k <= 4:
-                    group_t(pg, ph0, pn, "pe")
-                for f in w_at.get(k, ()):
-                    turn_w(f)
-                if k in (3, 4):
-                    group_x(k - 3)
-                if k == 4:
+            for k, (g, h0) in enumerate(order):
+                products(g, h0, 2, k in share)
+                f = None
+                if k > 0:
+                    pg, ph0 = order[k - 1]
+                    f = done(k - 1)
+                    style = how.get(k, "pool")
+                    if style == "pool":
+                        group_t(pg, ph0, 2, style)
+                    if k <= 0:
+                        for w in w_turn.get(k, ()):
+                            turn_w(w)
+                    if f is not None:
+                        turn_f(pg, f)
+                    if style != "pool":
+                        group_t(pg, ph0, 2, style)
+                if k > 0:
+                    for w in w_turn.get(k, ()):
+                        turn_w(w)
+                if k in xg:
+                    group_x(xg[k])
+                if k == 8:
                     turn_banks[:] = [1, 2]
-                for f in rows_at.get(k, ()):
-                    for j in range(4):
-                        mm_rows(rows[j], 0, f, j)
-                if k == 3:
-                    load_coefs(1)
-                if k == 5:
-                    for j in range(4):
-                        store_rows(rows[j], 0, j)
-                    tasks += [(6, rest_first, (0,)), (6, rest_first, (1,)), (0, store_rest, (0,))]
-                if k >= 6:
-                    for f in done[k - 2]:
-                        tasks += [(2, out1_tile, (f, a, "s")) for a in range(6)] + [(2, rest_second, (f,))]
-                room = {5: 12, 6: 22, 7: 22, 8: 10}.get(k, 0)
+                room = room_at.get(k, 9)
                 while tasks and room > 0:
                     cost, fn, args = tasks.pop(0)
                     fn(*args)
                     room -= cost
-                for f in done[k - 1]:
+                if k > 0:
+                    quant_t(pg, ph0, 2)
+                if k in xq:
+                    quant_x(xq[k])
+                add(g, h0, 2)
+                if f is not None:
                     quant_f(pg, f)
-                quant_t(pg, ph0, pn)
-                if k in (4, 5):
-                    quant_x(k - 4)
-                add(g, h0, n)
-                for f in w_at.get(k, ()):
-                    quant_w(f)
-            f = done[last - 1][0]
-            tasks += [(2, out1_tile, (f, a, "sv"[a % 2])) for a in range(6)] + [(2, rest_second, (f,))]
-            group_t(1, 14, 2, "last")
-            turn_f(1, 5, "sv")
+                for w in w_q.get(k, ()):
+                    quant_w(w)
+                if f is not None:
+                    if pg == 0 and f < 3:
+                        tasks.append((4, part_rows, (f,)))
+                        if f == 2:
+                            tasks += [(3, part_rest, (0,)), (3, part_rest, (1,))]
+                    else:
+                        if (pg, f) in ((1, 0), (1, 1), (1, 2), (0, 3), (0, 4)):
+                            tasks += [(2, out1_tile, (f, a, "s"[a % 1])) for a in range(6)]
+                        tasks.append((3, stream, (pg, f, 0 if pg else 3)))
+                        if pg == 1 and f >= 2:
+                            tasks.append((6, wide, (0, 2)) if f == 2 else (2, wide, (f, f)))
+                        if (pg, f) == (1, 5):
+                            tasks += [(0, finish_stream, (1, "ss")), (6, whole_row, (1, 3, 0, 5, "s")), (0, store_rest, (1,))]
+            group_t(0, 14, 2, "last")
+            turn_f(0, 5, "sv")
             for cost, fn, args in tasks:
                 fn(*args)
-            row0 = acc_tile(0)
-            for f in range(NPASS - 1):
-                mm_rows(row0, 1, f, 0)
-            quant_f(1, 5)
-            quant_t(1, 14, 2)
-            rest_second(5)
-            evac_rest([rest[1, 0], rest[1, 1]], 1, "sv")
-            mm_rows(row0, 1, 5, 0)
-            store_rows(row0, 1, 0, "s")
-            for a in range(6):
-                out1_tile(5, a, "vs"[a % 2])
-            store_rest(1, "sv")
+            quant_f(0, 5)
+            quant_t(0, 14, 2)
+            stream(0, 5, 3)
+            finish_stream(0, "vv")
+            for a in range(3):
+                out1_tile(5, a, "s")
+            store_rest(0, "vs")
             for j in (1, 2, 3):
-                acc = acc_tile((0, 4, 5)[j - 1])
-                for f in range(NPASS):
-                    mm_rows(acc, 1, f, j)
-                store_rows(acc, 1, j, "vsv"[j - 1])
+                whole_row(0, j, 3, (0, 3, 4)[j - 1], "v")
+            for a in range(3, 6):
+                out1_tile(5, a, "sv"[a % 2])

from contextlib import ExitStack

import concourse.mybir as mybir
from concourse.masks import make_identity

T, HID, HEADS, NOPE, ROPE = 1024, 768, 16, 64, 128
QK = NOPE + ROPE
HALF = ROPE // 2
F = HEADS * QK

FLOPS = 2 * 2 * T * HID * F

F32 = mybir.dt.float32
BF16 = mybir.dt.bfloat16
U32 = mybir.dt.uint32
U8 = mybir.dt.uint8
E4M3 = mybir.dt.float8_e4m3fn_x4
E5M2 = mybir.dt.float8_e5m2_x4
MULT = mybir.AluOpType.mult
ADD = mybir.AluOpType.add

P = 128
PACK = 4
KP = P * PACK
HP = 4
PF = HP * QK
NPASS = F // KP


def tile_multilatentattention_pb_v_kernel(
    tc, hidden_states, rope_cos, rope_sin, Wq, grad_out, out_0, out_1
):
    nc = tc.nc
    g_view = grad_out[0].rearrange("(g p j) h c -> g p j (h c)", p=P, j=PACK)
    x_view = hidden_states[0].rearrange("(g p j) h -> g p j h", p=P, j=PACK)
    cos_view = rope_cos.rearrange("(g p j) i -> p g (j i)", p=P, j=PACK)
    sin_view = rope_sin.rearrange("(g p j) i -> p g (j i)", p=P, j=PACK)
    out0_view = out_0[0].rearrange("(g p j) h -> g p j h", p=P, j=PACK)

    with ExitStack() as ctx:
        keep = ctx.enter_context(tc.tile_pool(name="keep", bufs=1))
        pool = ctx.enter_context(tc.tile_pool(name="pool", bufs=2))
        psum = ctx.enter_context(tc.psum_pool(name="psum", bufs=1))

        ident_f = keep.tile([P, P], F32, name="ident_f")
        ident_b = keep.tile([P, P], BF16, name="ident_b")
        make_identity(nc, ident_b[:])
        make_identity(nc, ident_f[:])

        cs = keep.tile([P, 2, 3, PACK * HALF], BF16, name="cs")
        nc.sync.dma_start(out=cs[:, :, 0, :], in_=cos_view)
        nc.sync.dma_start(out=cs[:, :, 1, :], in_=sin_view)
        nc.vector.tensor_scalar(
            out=cs[:, :, 2, :], in0=cs[:, :, 1, :], scalar1=-1.0, scalar2=None, op0=MULT
        )

        d_tiles = {}
        w_tiles = {}
        x_tiles = {}

        def load_heads(g, h0, n):
            fh = h0 // 8
            if h0 % 8 == 0:
                d_tiles[g, fh] = pool.tile([P, PACK, 2 * PF], BF16, name="d", bufs=2)
            c0 = (h0 % 8) * QK
            nc.sync.dma_start(
                out=d_tiles[g, fh][:, :, c0 : c0 + n * QK], in_=g_view[g, :, :, h0 * QK : (h0 + n) * QK]
            )

        def load_w(fh):
            for a in range(HID // P):
                w = pool.tile([P, F // 2], BF16, name="w_raw", bufs=6)
                nc.sync.dma_start(
                    out=w[:], in_=Wq[a * P : (a + 1) * P, fh * (F // 2) : (fh + 1) * (F // 2)]
                )
                w_tiles[fh, a] = w

        def load_x(g):
            x_tiles[g] = pool.tile([P, PACK, HID], BF16, name="x_raw", bufs=2)
            nc.sync.dma_start(out=x_tiles[g][:], in_=x_view[g])

        for h0 in range(0, 6, 2):
            load_heads(0, h0, 2)
        load_w(0)
        load_heads(0, 6, 2)
        load_heads(1, 0, 4)
        load_heads(1, 4, 4)
        load_w(1)
        load_x(0)
        load_x(1)
        load_heads(1, 8, 4)
        load_heads(1, 12, 4)
        load_heads(0, 8, 4)
        load_heads(0, 12, 4)

        w_codes = keep.tile([P, NPASS, HID], U32, name="w_codes", align_bytes=64)
        w_scales = keep.tile([P, NPASS, HID], U8, name="w_scales", align_bytes=64)
        x_codes = keep.tile([P, 2, HID], U32, name="x_codes", align_bytes=64)
        x_scales = keep.tile([P, 2, HID], U8, name="x_scales", align_bytes=64)
        t_codes = keep.tile([P, 2, F], U32, name="t_codes", align_bytes=64)
        t_scales = keep.tile([P, 2, F], U8, name="t_scales", align_bytes=64)

        def quantize(codes, scales, grouped, width, fmt):
            flat = grouped.rearrange("p c t -> p (c t)")
            c = 0
            while c < width:
                n = 512 if width - c >= 512 else 256
                nc.vector.quantize_mx(
                    out=codes[:, c : c + n].bitcast(fmt),
                    scales=scales[:, c : c + n],
                    in_=flat[:, c * PACK : (c + n) * PACK],
                )
                c += n

        w_grp, x_grp, t_grp, f_grp = {}, {}, {}, {}
        turn_banks = [1, 2, 3]
        turn_count = [0]

        def next_bank():
            i = turn_banks[turn_count[0] % len(turn_banks)]
            turn_count[0] += 1
            return f"b{i}"

        def tr_bank():
            return psum.tile([P, 2, 2, P], F32, name=next_bank(), bufs=1)

        def group_pe(grouped, src, width):
            flat = grouped[:].rearrange("p c j -> p (c j)")
            for c in range(0, width, 256):
                bank = psum.tile([P, 1024], BF16, name=next_bank(), bufs=1)
                for m in range(2):
                    nc.tensor.matmul(
                        bank[:, m * 512 : (m + 1) * 512], lhsT=ident_b[:],
                        rhs=src[:, :, c + m * P : c + (m + 1) * P].rearrange("p j c -> p c j"),
                        start=True, stop=True,
                    )
                nc.scalar.copy(out=flat[:, c * PACK : (c + 256) * PACK], in_=bank[:])

        def turn_w(f):
            grouped = pool.tile([P, HID, PACK], BF16, name="grp", bufs=4, align_bytes=64)
            words = grouped[:].rearrange("p c t -> p (c t)").bitcast(F32)
            for a0 in range(0, HID // P, 2):
                bank = tr_bank()
                for a in range(2):
                    src = w_tiles[f // 3, a0 + a][:].bitcast(F32)
                    for u in range(2):
                        lo = (f % 3) * 256 + u
                        nc.tensor.transpose(bank[:, a, u, :], src[:, lo : lo + 255 : 2], ident_f[:])
                nc.scalar.copy(
                    out=words[:, a0 * 256 : (a0 + 2) * 256].rearrange("p (a m u) -> p a m u", a=2, u=2),
                    in_=bank[:].rearrange("p a u m -> p a m u"),
                )
            w_grp[f] = grouped

        def quant_w(f):
            quantize(w_codes[:, f, :], w_scales[:, f, :], w_grp[f][:], HID, E4M3)

        def group_x(g):
            grouped = pool.tile([P, HID, PACK], BF16, name="grp", bufs=4, align_bytes=64)
            for c in range(0, HID, 128):
                nc.scalar.copy(
                    out=grouped[:, c : c + 128, :],
                    in_=x_tiles[g][:, :, c : c + 128].rearrange("p j c -> p c j"),
                )
            x_grp[g] = grouped

        def quant_x(g):
            quantize(x_codes[:, g, :], x_scales[:, g, :], x_grp[g][:], HID, E4M3)

        cs_bank = psum.tile([P, 2, 2, PACK, HALF], BF16, name="b0", bufs=1)
        for g in range(2):
            nc.tensor.matmul(
                cs_bank[:, g].rearrange("p k j i -> p (k j i)"), lhsT=ident_b[:],
                rhs=cs[:, g, 0:2, :].rearrange("p k w -> p (k w)"), start=True, stop=True,
            )

        prod = {}

        def rope_view(g, h0, n):
            d = d_tiles[g, h0 // 8][:].rearrange("p j (h c) -> p j h c", c=QK)
            r = d[:, :, h0 % 8 : h0 % 8 + n, NOPE:QK]
            return r.rearrange("p j h (i e) -> p j h i e", e=2)

        def products(g, h0, n, share=False):
            r = rope_view(g, h0, n)

            def coef(k):
                return cs_bank[:, g, k, :, :].unsqueeze(2).to_broadcast([P, PACK, n, HALF])

            pc = pool.tile([P, 2, PACK, n, HALF], F32, name="pc", bufs=2)
            ps = pool.tile([P, 2, PACK, n, HALF], F32, name="ps", bufs=2)
            minus_sin = cs[:, g, 2, :].rearrange("p (j i) -> p j i", i=HALF).unsqueeze(2)
            eng = nc.gpsimd if share else nc.vector

            def minus():
                eng.tensor_tensor(
                    out=ps[:, 1], in0=r[:, :, :, :, 0],
                    in1=minus_sin.to_broadcast([P, PACK, n, HALF]), op=MULT,
                )

            if share:
                minus()
            for e in range(2):
                nc.vector.tensor_tensor(out=pc[:, e], in0=r[:, :, :, :, e], in1=coef(0), op=MULT)
            nc.vector.tensor_tensor(out=ps[:, 0], in0=r[:, :, :, :, 1], in1=coef(1), op=MULT)
            if not share:
                minus()
            prod[g, h0] = pc, ps

        def add(g, h0, n):
            pc, ps = prod[g, h0]
            nc.vector.tensor_tensor(
                out=rope_view(g, h0, n), in0=pc[:].rearrange("p e j h i -> p j h i e"),
                in1=ps[:].rearrange("p e j h i -> p j h i e"), op=ADD,
            )

        f_codes, f_scales = {}, {}

        def copy_words(eng, words, bank, c):
            out = words[:, c * 256 : (c + 2) * 256].rearrange("p (a m u) -> p a m u", a=2, u=2)
            in_ = bank[:].rearrange("p a u m -> p a m u")
            if eng == "v":
                nc.vector.tensor_copy(out=out, in_=in_)
            else:
                nc.scalar.copy(out=out, in_=in_)

        def turn_f(g, f, engs="ss"):
            grouped = pool.tile([P, KP, PACK], BF16, name="fgrp", bufs=3, align_bytes=64)
            words = grouped[:].rearrange("p c t -> p (c t)").bitcast(F32)
            d = d_tiles[g, f // 3]
            for j0 in range(0, PACK, 2):
                bank = tr_bank()
                for j in range(2):
                    src = d[:, j0 + j, :].bitcast(F32)
                    for u in range(2):
                        lo = (f % 3) * 256 + u
                        nc.tensor.transpose(bank[:, j, u, :], src[:, lo : lo + 255 : 2], ident_f[:])
                copy_words(engs[j0 // 2], words, bank, j0)
            f_grp[g, f] = grouped

        def quant_f(g, f):
            fc = pool.tile([P, KP], U32, name="f_codes", bufs=9, align_bytes=64)
            fs = pool.tile([P, KP], U8, name="f_scales", bufs=9, align_bytes=64)
            quantize(fc[:], fs[:], f_grp[g, f][:], KP, E5M2)
            f_codes[g, f], f_scales[g, f] = fc, fs

        def group_t(g, h0, n, how):
            grouped = pool.tile([P, n * QK, PACK], BF16, name="grp", bufs=4, align_bytes=64)
            c0 = (h0 % 8) * QK
            raw = d_tiles[g, h0 // 8][:, :, c0 : c0 + n * QK]
            src = raw.rearrange("p j c -> p c j")
            w = n * QK
            if how == "pe":
                group_pe(grouped, raw, w)
            elif how == "last":
                nc.vector.tensor_copy(out=grouped[:, 0:256, :], in_=src[:, 0:256, :])
                nc.scalar.copy(out=grouped[:, 256:w, :], in_=src[:, 256:w, :])
            else:
                m = 288
                nc.gpsimd.tensor_scalar(
                    out=grouped[:, 0:m, :], in0=src[:, 0:m, :], scalar1=1.0, scalar2=0.0, op0=MULT, op1=ADD
                )
                if m < w:
                    nc.scalar.copy(out=grouped[:, m:w, :], in_=src[:, m:w, :])
            t_grp[g, h0] = grouped

        def quant_t(g, h0, n):
            cols = slice(h0 * QK, (h0 + n) * QK)
            w = n * QK
            codes, scales = t_codes[:, g, cols], t_scales[:, g, cols]
            grouped = t_grp[g, h0]
            if w == 384:
                flat = grouped[:].rearrange("p c t -> p (c t)")
                for c, m in ((0, 256), (256, 128)):
                    nc.vector.quantize_mx(
                        out=codes[:, c : c + m].bitcast(E5M2), scales=scales[:, c : c + m],
                        in_=flat[:, c * PACK : (c + m) * PACK],
                    )
            else:
                quantize(codes, scales, grouped[:], w, E5M2)

        def mm_rows(acc, g, f, j, first, final):
            m = slice(j * P, (j + 1) * P)
            nc.tensor.matmul_mx(
                out=acc[:], lhsT=f_codes[g, f][:, m].bitcast(E5M2), lhsT_scale=f_scales[g, f][:, m],
                rhs=w_codes[:, f, 0:512].bitcast(E4M3), rhs_scale=w_scales[:, f, 0:512],
                start=(f == first), stop=(f == final),
            )

        def mm_rest(acc, g, f, b, first, final):
            m = slice(512 + b * P, 512 + (b + 1) * P)
            nc.tensor.matmul_mx(
                out=acc[:], lhsT=w_codes[:, f, m].bitcast(E4M3), lhsT_scale=w_scales[:, f, m],
                rhs=f_codes[g, f][:].bitcast(E5M2), rhs_scale=f_scales[g, f][:],
                start=(f == first), stop=(f == final),
            )

        def acc_tile(i):
            return psum.tile([P, 512], F32, name=f"b{i}", bufs=1)

        def evac(eng, out, in_):
            if eng == "v":
                nc.vector.tensor_copy(out=out, in_=in_)
            else:
                nc.scalar.copy(out=out, in_=in_)

        spill = {}

        def evac_sum(eng, out, in_, g, i):
            if g == 0:
                nc.vector.tensor_tensor(out=out, in0=in_, in1=spill[i][:], op=ADD)
            else:
                evac(eng, out, in_)

        def store_rows(acc, g, j, eng="s"):
            o = pool.tile([P, 512], F32, name="o_stage", bufs=6)
            evac_sum(eng, o[:], acc[:], g, j)
            nc.sync.dma_start(out=out0_view[g, :, j, 0:512], in_=o[:])

        rest_sb = {}

        def evac_rest(acc2, g, engs="ss"):
            rest_sb[g] = []
            for b in range(2):
                ot = pool.tile([P, 512], F32, name="ot", bufs=2)
                evac_sum(engs[b], ot[:], acc2[b][:], g, 4 + b)
                rest_sb[g].append(ot)

        def store_rest(g, engs="ss"):
            rest = pool.tile([P, PACK, 256], F32, name="rest", bufs=1)
            for j0 in range(0, PACK, 2):
                bank = tr_bank()
                for j in range(2):
                    for b in range(2):
                        nc.tensor.transpose(
                            bank[:, j, b, :], rest_sb[g][b][:, (j0 + j) * P : (j0 + j + 1) * P], ident_f[:]
                        )
                evac(
                    engs[j0 // 2], rest[:, j0 : j0 + 2, :].rearrange("p a c -> p (a c)"),
                    bank[:].rearrange("p a b m -> p (a b m)"),
                )
            nc.sync.dma_start(out=out0_view[g, :, :, 512:HID], in_=rest[:])

        out_banks = [6, 7]
        out_count = [0]

        def out1_tile(f, a, eng):
            cols = slice(f * 512, (f + 1) * 512)
            acc = acc_tile(out_banks[out_count[0] % len(out_banks)])
            out_count[0] += 1
            for g in range(2):
                nc.tensor.matmul_mx(
                    out=acc[:], lhsT=x_codes[:, g, a * P : (a + 1) * P].bitcast(E4M3),
                    lhsT_scale=x_scales[:, g, a * P : (a + 1) * P],
                    rhs=t_codes[:, g, cols].bitcast(E5M2), rhs_scale=t_scales[:, g, cols],
                    start=(g == 0), stop=(g == 1),
                )
            o = pool.tile([P, 512], F32, name="o_stage", bufs=6)
            evac(eng, o[:], acc[:])
            nc.sync.dma_start(out=out_1[a * P : (a + 1) * P, cols], in_=o[:])

        order = [(g, fh * 8 + h) for g, fh in ((0, 0), (1, 0), (1, 1), (0, 1)) for h in range(0, 8, 2)]
        how = {}
        share = []
        w_turn = {1: [0], 2: [1], 3: [2], 5: [3], 6: [4], 7: [5]}
        w_q = {1: [0], 2: [1], 3: [2], 5: [3], 6: [4], 7: [5]}
        xg = {4: 0, 5: 1}
        xq = {5: 0, 6: 1}
        room_at = {13: 10, 14: 12, 15: 20}
        acc = {}
        tasks = []
        fresh_w, fresh_f = set(), {}

        def done(k):
            return (order[k][1] // 8) * 3 + k % 4 - 1 if k % 4 else None

        def part_rows(f):
            for j in range(4):
                if f == 0:
                    acc["part", j] = acc_tile(4 + j)
                mm_rows(acc["part", j], 0, f, j, 0, 2)
            if f == 2:
                for j in range(4):
                    spill[j] = keep.tile([P, 512], F32, name=f"spill{j}")
                    evac("s", spill[j][:], acc["part", j][:])

        def part_rest(b):
            a = acc_tile(4 + b)
            for f in range(3):
                mm_rest(a, 0, f, b, 0, 2)
            spill[4 + b] = keep.tile([P, 512], F32, name=f"spill{4 + b}")
            evac("s", spill[4 + b][:], a[:])

        def stream(g, f, first):
            for b in range(2):
                if f == first:
                    acc[g, "rest", b] = acc_tile(3 + b)
                mm_rest(acc[g, "rest", b], g, f, b, first, 5)
            if f == first:
                acc[g, 0] = acc_tile(5)
            mm_rows(acc[g, 0], g, f, 0, first, 5)

        def wide(f0, f1):
            for j in (1, 2):
                if f0 == 0:
                    acc[1, j] = acc_tile(5 + j)
                for f in range(f0, f1 + 1):
                    mm_rows(acc[1, j], 1, f, j, 0, 5)
                if f1 == 5:
                    store_rows(acc[1, j], 1, j, "s")

        def finish_stream(g, engs):
            evac_rest([acc[g, "rest", 0], acc[g, "rest", 1]], g, engs)
            store_rows(acc[g, 0], g, 0, engs[0])

        def whole_row(g, j, first, bank, eng):
            a = acc_tile(bank)
            for f in range(first, NPASS):
                mm_rows(a, g, f, j, first, 5)
            store_rows(a, g, j, eng)

        with tc.manual_schedule():
            for k, (g, h0) in enumerate(order):
                products(g, h0, 2, k in share)
                f = None
                if k > 0:
                    pg, ph0 = order[k - 1]
                    f = done(k - 1)
                    style = how.get(k, "pool")
                    if style == "pool":
                        group_t(pg, ph0, 2, style)
                    if k <= 0:
                        for w in w_turn.get(k, ()):
                            turn_w(w)
                    if f is not None:
                        turn_f(pg, f)
                    if style != "pool":
                        group_t(pg, ph0, 2, style)
                if k > 0:
                    for w in w_turn.get(k, ()):
                        turn_w(w)
                if k in xg:
                    group_x(xg[k])
                if k == 8:
                    turn_banks[:] = [1, 2]
                room = room_at.get(k, 9)
                while tasks and room > 0:
                    cost, fn, args = tasks.pop(0)
                    fn(*args)
                    room -= cost
                if k > 0:
                    quant_t(pg, ph0, 2)
                if k in xq:
                    quant_x(xq[k])
                add(g, h0, 2)
                if f is not None:
                    quant_f(pg, f)
                for w in w_q.get(k, ()):
                    quant_w(w)
                if f is not None:
                    if pg == 0 and f < 3:
                        tasks.append((4, part_rows, (f,)))
                        if f == 2:
                            tasks += [(3, part_rest, (0,)), (3, part_rest, (1,))]
                    else:
                        if (pg, f) in ((1, 0), (1, 1), (1, 2), (0, 3), (0, 4)):
                            tasks += [(2, out1_tile, (f, a, "s"[a % 1])) for a in range(6)]
                        tasks.append((3, stream, (pg, f, 0 if pg else 3)))
                        if pg == 1 and f >= 2:
                            tasks.append((6, wide, (0, 2)) if f == 2 else (2, wide, (f, f)))
                        if (pg, f) == (1, 5):
                            tasks += [(0, finish_stream, (1, "ss")), (6, whole_row, (1, 3, 0, 5, "s")), (0, store_rest, (1,))]
            group_t(0, 14, 2, "last")
            turn_f(0, 5, "sv")
            for cost, fn, args in tasks:
                fn(*args)
            quant_f(0, 5)
            quant_t(0, 14, 2)
            stream(0, 5, 3)
            finish_stream(0, "vv")
            for a in range(3):
                out1_tile(5, a, "s")
            store_rest(0, "vs")
            for j in (1, 2, 3):
                whole_row(0, j, 3, (0, 3, 4)[j - 1], "v")
            for a in range(3, 6):
                out1_tile(5, a, "sv"[a % 2])
